import numpy as np
import ml_dtypes


def mxq(x, axis, fmt="e4m3"):
    dtype, down = {"e4m3": (ml_dtypes.float8_e4m3fn, 7), "e5m2": (ml_dtypes.float8_e5m2, 14)}[fmt]
    v = np.moveaxis(np.asarray(x, np.float32).astype(ml_dtypes.bfloat16).astype(np.float64), axis, -1)
    blocks = v.reshape(v.shape[:-1] + (-1, 32))
    amax = np.abs(blocks).max(-1, keepdims=True)
    byte = np.maximum(np.where(amax > 0, np.frexp(amax)[1] - 1 + 127, 0) - down, 1)
    scale = np.exp2(byte - 127.0)
    codes = (blocks / scale).astype(np.float32).astype(dtype).astype(np.float64)
    return np.moveaxis((codes * scale).reshape(v.shape), -1, axis)


WIDE = False


def mx_kscale(k):
    if not WIDE:
        return np.ones(k)
    levels = np.array([20, -20, 10, -10, 0])
    a = np.random.permutation(np.resize(levels, k // 512 * 4)).reshape(k // 512, 4)
    idx = np.arange(k)
    return np.exp2(a[idx // 512, idx % 128 // 32])


BF16 = ml_dtypes.bfloat16


def bf(x):
    return np.asarray(x, np.float32).astype(BF16)


def f64(x):
    return np.asarray(x).astype(np.float64)


B, F, G, N, L = 512, 128, 256, 100, 1
S2 = (L + 1) ** 2
C = sum((2 * l + 1) ** 2 for l in range(L + 1))


def setup_inputs():
    k = mx_kscale(B)
    x = np.random.standard_normal((B, F, S2)) * k[:, None, None]
    psi = np.random.standard_normal((G, F, S2))
    g = np.random.standard_normal((G, B, C)) * np.exp2(np.random.randint(-12, 1, (1, B, 1))) * 4.0 / k[None, :, None]
    return {"x": bf(x), "psi": bf(psi), "grad_out": bf(g)}


def reference(x, psi, grad_out):
    xq = mxq(f64(x), 0, "e4m3")
    gq = mxq(f64(grad_out), 1, "e5m2")
    scale = 1.0 / np.sqrt(F)
    outs = []
    c = 0
    for l in range(L + 1):
        s, d = l * l, 2 * l + 1
        a = xq[:, :, s:s + d].transpose(1, 2, 0).reshape(F, d * B)
        p = gq[:, :, c:c + d * d].reshape(G, B, d, d).transpose(2, 1, 0, 3).reshape(d * B, G * d)
        o = scale * (a @ p)
        outs.append(o.reshape(F, G, d).transpose(1, 0, 2))
        c += d * d
    return np.concatenate(outs, axis=-1)

@@ -1,0 +1,127 @@
+import math
+from contextlib import ExitStack
+
+import concourse.mybir as mybir
+from concourse.masks import make_identity
+
+F32 = mybir.dt.float32
+BF16 = mybir.dt.bfloat16
+U32 = mybir.dt.uint32
+U8 = mybir.dt.uint8
+E4M3X4 = mybir.dt.float8_e4m3fn_x4
+E5M2X4 = mybir.dt.float8_e5m2_x4
+
+P = 128
+PACK = 4
+B, F, G, S2, C = 512, 128, 256, 4, 10
+PAIRS = C // 2
+CHUNK_G = P // PACK
+CHUNKS_PER_TILE = P // CHUNK_G
+G_TILES = G // P
+SCALAR_PAIRS = 3
+WINDOW = 4 * P
+
+FLOPS = 2 * B * F * G * C
+BYTES = 2 * B * F * S2 + 2 * G * B * C + 4 * G * F * S2
+
+
+def tile_s2conv_pa_s_kernel(tc, x, psi, grad_out, out):
+    nc = tc.nc
+    scale = 1.0 / math.sqrt(F)
+
+    with ExitStack() as ctx:
+        keep = ctx.enter_context(tc.tile_pool(name="keep", bufs=1))
+        loads = ctx.enter_context(tc.tile_pool(name="loads", bufs=G_TILES * CHUNKS_PER_TILE))
+        tiles = ctx.enter_context(tc.tile_pool(name="tiles", bufs=G_TILES))
+        flips = ctx.enter_context(tc.psum_pool(name="flips", bufs=2))
+        sums = ctx.enter_context(tc.psum_pool(name="sums", bufs=1))
+
+        x_raw = keep.tile([P, PACK, F * S2], BF16)
+        nc.sync.dma_start(out=x_raw[:], in_=x.rearrange("(t p) f s -> p t (f s)", p=P))
+        chunk_rows = grad_out.rearrange("(n g) (t b) c -> n (g t) (b c)", g=CHUNK_G, t=PACK)
+        raws = []
+        for n in range(G_TILES * CHUNKS_PER_TILE):
+            raw = loads.tile([P, P * C], BF16)
+            nc.sync.dma_start(out=raw[:], in_=chunk_rows[n])
+            raws.append(raw)
+
+        ident = keep.tile([P, P], F32)
+        make_identity(nc, ident[:])
+
+        x_grouped = keep.tile([P, S2 * F * PACK], BF16, align_bytes=64)
+        nc.vector.tensor_copy(
+            out=x_grouped[:].rearrange("p (s f t) -> p s f t", s=S2, t=PACK),
+            in_=x_raw[:].rearrange("p t (f s) -> p s f t", s=S2),
+        )
+        x_words = keep.tile([P, S2 * F], U32, align_bytes=64)
+        x_scales = keep.tile([P, S2 * F], U8, align_bytes=64)
+        nc.vector.quantize_mx(out=x_words[:].bitcast(E4M3X4), scales=x_scales[:], in_=x_grouped[:])
+
+        for gt in range(G_TILES):
+            g_grouped = tiles.tile([P, C * P * PACK], BF16, align_bytes=64)
+            grouped_view = g_grouped[:].rearrange("p (c g t) -> p c g t", c=C, t=PACK)
+            for i in range(CHUNKS_PER_TILE):
+                raw = raws[gt * CHUNKS_PER_TILE + i]
+                pair_cols = raw[:].bitcast(F32).rearrange("q (b w) -> q w b", w=PAIRS)
+                features = slice(i * CHUNK_G, (i + 1) * CHUNK_G)
+                for engine_copy, first, count in (
+                    (nc.scalar.copy, 0, SCALAR_PAIRS),
+                    (nc.vector.tensor_copy, SCALAR_PAIRS, PAIRS - SCALAR_PAIRS),
+                ):
+                    flipped = flips.tile([P, 4 * P], F32, tag="flip%d" % first)
+                    for j in range(count):
+                        nc.tensor.transpose(
+                            flipped[:, j * P : (j + 1) * P], pair_cols[:, first + j, :], ident[:]
+                        )
+                    engine_copy(
+                        out=grouped_view[:, 2 * first : 2 * (first + count), features, :].rearrange(
+                            "p (w e) g t -> p w e (g t)", e=2
+                        ),
+                        in_=flipped[:].bitcast(BF16)[:, : 2 * count * P].rearrange(
+                            "p (w k e) -> p w e k", w=count, e=2
+                        ),
+                    )
+
+            g_words = tiles.tile([P, C * P], U32, align_bytes=64)
+            g_scales = tiles.tile([P, C * P], U8, align_bytes=64)
+            for w in range(PAIRS):
+                cols = slice(2 * w * P, 2 * (w + 1) * P)
+                nc.vector.quantize_mx(
+                    out=g_words[:, cols].bitcast(E5M2X4),
+                    scales=g_scales[:, cols],
+                    in_=g_grouped[:, 2 * w * P * PACK : 2 * (w + 1) * P * PACK],
+                )
+
+            def multiply(acc, s, first_c, start, stop):
+                window = slice(first_c * P, first_c * P + WINDOW)
+                nc.tensor.matmul_mx(
+                    out=acc[:],
+                    lhsT=x_words[:, s * F : (s + 1) * F].bitcast(E4M3X4),
+                    lhsT_scale=x_scales[:, s * F : (s + 1) * F],
+                    rhs=g_words[:, window].bitcast(E5M2X4),
+                    rhs_scale=g_scales[:, window],
+                    start=start,
+                    stop=stop,
+                )
+
+            acc0 = sums.tile([P, WINDOW], F32)
+            multiply(acc0, 0, 0, True, True)
+            acc1 = sums.tile([P, WINDOW], F32)
+            for u in range(3):
+                multiply(acc1, 1 + u, 3 * u, u == 0, u == 2)
+
+            scaled = tiles.tile([P, S2 * P], F32)
+            nc.vector.tensor_scalar_mul(out=scaled[:, :P], in0=acc0[:, :P], scalar1=scale)
+            nc.scalar.mul(out=scaled[:, P:], in_=acc1[:, P:], mul=scale)
+
+            back = sums.tile([P, S2 * F], F32)
+            for s in range(S2):
+                nc.tensor.transpose(back[:, s * F : (s + 1) * F], scaled[:, s * P : (s + 1) * P], ident[:])
+            result = tiles.tile([P, F * S2], F32)
+            nc.scalar.copy(
+                out=result[:].rearrange("p (f s) -> p f s", s=S2),
+                in_=back[:].rearrange("p (s f) -> p f s", s=S2),
+            )
+            nc.sync.dma_start(
+                out=out[gt * P : (gt + 1) * P].rearrange("g f s -> g (f s)"), in_=result[:]
+            )

@@ -10,6 +10,8 @@ U32 = mybir.dt.uint32
 U8 = mybir.dt.uint8
 E4M3X4 = mybir.dt.float8_e4m3fn_x4
 E5M2X4 = mybir.dt.float8_e5m2_x4
+MULT = mybir.AluOpType.mult
+ADD = mybir.AluOpType.add
 
 P = 128
 PACK = 4
@@ -18,7 +20,12 @@ PAIRS = C // 2
 CHUNK_G = P // PACK
 CHUNKS_PER_TILE = P // CHUNK_G
 G_TILES = G // P
+CHUNKS = G_TILES * CHUNKS_PER_TILE
+CHUNKS_BEFORE_X = 2
 SCALAR_PAIRS = 3
+QUANT_CHUNKS = 2
+QUANT_G = QUANT_CHUNKS * CHUNK_G
+PSUM_BANKS = 8
 WINDOW = 4 * P
 
 FLOPS = 2 * B * F * G * C
@@ -31,97 +38,108 @@ def tile_s2conv_pa_s_kernel(tc, x, psi, grad_out, out):
 
     with ExitStack() as ctx:
         keep = ctx.enter_context(tc.tile_pool(name="keep", bufs=1))
-        loads = ctx.enter_context(tc.tile_pool(name="loads", bufs=G_TILES * CHUNKS_PER_TILE))
+        loads = ctx.enter_context(tc.tile_pool(name="loads", bufs=CHUNKS))
         tiles = ctx.enter_context(tc.tile_pool(name="tiles", bufs=G_TILES))
-        flips = ctx.enter_context(tc.psum_pool(name="flips", bufs=2))
-        sums = ctx.enter_context(tc.psum_pool(name="sums", bufs=1))
-
-        x_raw = keep.tile([P, PACK, F * S2], BF16)
-        nc.sync.dma_start(out=x_raw[:], in_=x.rearrange("(t p) f s -> p t (f s)", p=P))
-        chunk_rows = grad_out.rearrange("(n g) (t b) c -> n (g t) (b c)", g=CHUNK_G, t=PACK)
-        raws = []
-        for n in range(G_TILES * CHUNKS_PER_TILE):
-            raw = loads.tile([P, P * C], BF16)
-            nc.sync.dma_start(out=raw[:], in_=chunk_rows[n])
-            raws.append(raw)
+        banks = ctx.enter_context(tc.psum_pool(name="banks", bufs=PSUM_BANKS))
+        ctx.enter_context(tc.manual_schedule())
 
         ident = keep.tile([P, P], F32)
         make_identity(nc, ident[:])
 
+        chunk_rows = grad_out.rearrange("(n g) (t b) c -> n (g t) (b c)", g=CHUNK_G, t=PACK)
+        x_raw = keep.tile([P, PACK, F * S2], BF16)
+        pair_cols = []
+        for n in range(CHUNKS):
+            if n == CHUNKS_BEFORE_X:
+                nc.sync.dma_start(out=x_raw[:], in_=x.rearrange("(t p) f s -> p t (f s)", p=P))
+            raw = loads.tile([P, P * C], BF16)
+            nc.sync.dma_start(out=raw[:], in_=chunk_rows[n])
+            pair_cols.append(raw[:].bitcast(F32).rearrange("q (b w) -> q w b", w=PAIRS))
+
         x_grouped = keep.tile([P, S2 * F * PACK], BF16, align_bytes=64)
-        nc.vector.tensor_copy(
+        nc.gpsimd.tensor_scalar(
             out=x_grouped[:].rearrange("p (s f t) -> p s f t", s=S2, t=PACK),
-            in_=x_raw[:].rearrange("p t (f s) -> p s f t", s=S2),
+            in0=x_raw[:].rearrange("p t (f s) -> p s f t", s=S2),
+            scalar1=1.0,
+            scalar2=0.0,
+            op0=MULT,
+            op1=ADD,
         )
         x_words = keep.tile([P, S2 * F], U32, align_bytes=64)
         x_scales = keep.tile([P, S2 * F], U8, align_bytes=64)
-        nc.vector.quantize_mx(out=x_words[:].bitcast(E4M3X4), scales=x_scales[:], in_=x_grouped[:])
 
+        def flip(chunk, first, count):
+            bank = banks.tile([P, WINDOW], F32)
+            for j in range(count):
+                nc.tensor.transpose(bank[:, j * P : (j + 1) * P], chunk[:, first + j, :], ident[:])
+            return bank[:].bitcast(BF16)[:, : 2 * count * P].rearrange("p (w k e) -> p w e k", w=count, e=2)
+
+        g_words = []
+        g_scales = []
         for gt in range(G_TILES):
             g_grouped = tiles.tile([P, C * P * PACK], BF16, align_bytes=64)
-            grouped_view = g_grouped[:].rearrange("p (c g t) -> p c g t", c=C, t=PACK)
+            grouped_view = g_grouped[:].rearrange("p (w e g t) -> p w e g t", w=PAIRS, e=2, t=PACK)
+            words = tiles.tile([P, C * P], U32, align_bytes=64)
+            scales = tiles.tile([P, C * P], U8, align_bytes=64)
             for i in range(CHUNKS_PER_TILE):
-                raw = raws[gt * CHUNKS_PER_TILE + i]
-                pair_cols = raw[:].bitcast(F32).rearrange("q (b w) -> q w b", w=PAIRS)
+                chunk = pair_cols[gt * CHUNKS_PER_TILE + i]
                 features = slice(i * CHUNK_G, (i + 1) * CHUNK_G)
-                for engine_copy, first, count in (
-                    (nc.scalar.copy, 0, SCALAR_PAIRS),
-                    (nc.vector.tensor_copy, SCALAR_PAIRS, PAIRS - SCALAR_PAIRS),
-                ):
-                    flipped = flips.tile([P, 4 * P], F32, tag="flip%d" % first)
-                    for j in range(count):
-                        nc.tensor.transpose(
-                            flipped[:, j * P : (j + 1) * P], pair_cols[:, first + j, :], ident[:]
+                for_scalar = flip(chunk, 0, SCALAR_PAIRS)
+                for_vector = flip(chunk, SCALAR_PAIRS, PAIRS - SCALAR_PAIRS)
+                nc.scalar.copy(
+                    out=grouped_view[:, :SCALAR_PAIRS, :, features, :].rearrange("p w e g t -> p w e (g t)"),
+                    in_=for_scalar,
+                )
+                nc.vector.tensor_copy(
+                    out=grouped_view[:, SCALAR_PAIRS:, :, features, :].rearrange("p w e g t -> p w e (g t)"),
+                    in_=for_vector,
+                )
+                if (i + 1) % QUANT_CHUNKS == 0:
+                    for c in range(C):
+                        first_col = c * P + (i + 1) * CHUNK_G - QUANT_G
+                        cols = slice(first_col, first_col + QUANT_G)
+                        nc.vector.quantize_mx(
+                            out=words[:, cols].bitcast(E5M2X4),
+                            scales=scales[:, cols],
+                            in_=g_grouped[:, first_col * PACK : (first_col + QUANT_G) * PACK],
                         )
-                    engine_copy(
-                        out=grouped_view[:, 2 * first : 2 * (first + count), features, :].rearrange(
-                            "p (w e) g t -> p w e (g t)", e=2
-                        ),
-                        in_=flipped[:].bitcast(BF16)[:, : 2 * count * P].rearrange(
-                            "p (w k e) -> p w e k", w=count, e=2
-                        ),
-                    )
+            g_words.append(words)
+            g_scales.append(scales)
+            if gt == 0:
+                nc.vector.quantize_mx(out=x_words[:].bitcast(E4M3X4), scales=x_scales[:], in_=x_grouped[:])
 
-            g_words = tiles.tile([P, C * P], U32, align_bytes=64)
-            g_scales = tiles.tile([P, C * P], U8, align_bytes=64)
-            for w in range(PAIRS):
-                cols = slice(2 * w * P, 2 * (w + 1) * P)
-                nc.vector.quantize_mx(
-                    out=g_words[:, cols].bitcast(E5M2X4),
-                    scales=g_scales[:, cols],
-                    in_=g_grouped[:, 2 * w * P * PACK : 2 * (w + 1) * P * PACK],
-                )
+        def multiply(acc, gt, s, first_c, start, stop):
+            window = slice(first_c * P, first_c * P + WINDOW)
+            nc.tensor.matmul_mx(
+                out=acc[:],
+                lhsT=x_words[:, s * F : (s + 1) * F].bitcast(E4M3X4),
+                lhsT_scale=x_scales[:, s * F : (s + 1) * F],
+                rhs=g_words[gt][:, window].bitcast(E5M2X4),
+                rhs_scale=g_scales[gt][:, window],
+                start=start,
+                stop=stop,
+            )
 
-            def multiply(acc, s, first_c, start, stop):
-                window = slice(first_c * P, first_c * P + WINDOW)
-                nc.tensor.matmul_mx(
-                    out=acc[:],
-                    lhsT=x_words[:, s * F : (s + 1) * F].bitcast(E4M3X4),
-                    lhsT_scale=x_scales[:, s * F : (s + 1) * F],
-                    rhs=g_words[:, window].bitcast(E5M2X4),
-                    rhs_scale=g_scales[:, window],
-                    start=start,
-                    stop=stop,
-                )
-
-            acc0 = sums.tile([P, WINDOW], F32)
-            multiply(acc0, 0, 0, True, True)
-            acc1 = sums.tile([P, WINDOW], F32)
+        scaled_sums = []
+        for gt in range(G_TILES):
+            acc0 = banks.tile([P, WINDOW], F32, tag="bank")
+            multiply(acc0, gt, 0, 0, True, True)
+            acc1 = banks.tile([P, WINDOW], F32, tag="bank")
             for u in range(3):
-                multiply(acc1, 1 + u, 3 * u, u == 0, u == 2)
-
+                multiply(acc1, gt, 1 + u, 3 * u, u == 0, u == 2)
             scaled = tiles.tile([P, S2 * P], F32)
             nc.vector.tensor_scalar_mul(out=scaled[:, :P], in0=acc0[:, :P], scalar1=scale)
             nc.scalar.mul(out=scaled[:, P:], in_=acc1[:, P:], mul=scale)
+            scaled_sums.append(scaled)
 
-            back = sums.tile([P, S2 * F], F32)
+        for gt in range(G_TILES):
+            back = banks.tile([P, S2 * F], F32, tag="bank")
             for s in range(S2):
-                nc.tensor.transpose(back[:, s * F : (s + 1) * F], scaled[:, s * P : (s + 1) * P], ident[:])
+                nc.tensor.transpose(back[:, s * F : (s + 1) * F], scaled_sums[gt][:, s * P : (s + 1) * P], ident[:])
             result = tiles.tile([P, F * S2], F32)
-            nc.scalar.copy(
+            last_copy = nc.vector.tensor_copy if gt % 2 == 0 else nc.scalar.copy
+            last_copy(
                 out=result[:].rearrange("p (f s) -> p f s", s=S2),
                 in_=back[:].rearrange("p (s f) -> p f s", s=S2),
             )
-            nc.sync.dma_start(
-                out=out[gt * P : (gt + 1) * P].rearrange("g f s -> g (f s)"), in_=result[:]
-            )
+            nc.sync.dma_start(out=out[gt * P : (gt + 1) * P].rearrange("g f s -> g (f s)"), in_=result[:])

@@ -10,8 +10,6 @@ U32 = mybir.dt.uint32
 U8 = mybir.dt.uint8
 E4M3X4 = mybir.dt.float8_e4m3fn_x4
 E5M2X4 = mybir.dt.float8_e5m2_x4
-MULT = mybir.AluOpType.mult
-ADD = mybir.AluOpType.add
 
 P = 128
 PACK = 4
@@ -21,7 +19,6 @@ CHUNK_G = P // PACK
 CHUNKS_PER_TILE = P // CHUNK_G
 G_TILES = G // P
 CHUNKS = G_TILES * CHUNKS_PER_TILE
-CHUNKS_BEFORE_X = 2
 SCALAR_PAIRS = 3
 QUANT_CHUNKS = 2
 QUANT_G = QUANT_CHUNKS * CHUNK_G
@@ -48,25 +45,21 @@ def tile_s2conv_pa_s_kernel(tc, x, psi, grad_out, out):
 
         chunk_rows = grad_out.rearrange("(n g) (t b) c -> n (g t) (b c)", g=CHUNK_G, t=PACK)
         x_raw = keep.tile([P, PACK, F * S2], BF16)
+        nc.sync.dma_start(out=x_raw[:], in_=x.rearrange("(t p) f s -> p t (f s)", p=P))
         pair_cols = []
         for n in range(CHUNKS):
-            if n == CHUNKS_BEFORE_X:
-                nc.sync.dma_start(out=x_raw[:], in_=x.rearrange("(t p) f s -> p t (f s)", p=P))
             raw = loads.tile([P, P * C], BF16)
             nc.sync.dma_start(out=raw[:], in_=chunk_rows[n])
             pair_cols.append(raw[:].bitcast(F32).rearrange("q (b w) -> q w b", w=PAIRS))
 
         x_grouped = keep.tile([P, S2 * F * PACK], BF16, align_bytes=64)
-        nc.gpsimd.tensor_scalar(
+        nc.vector.tensor_copy(
             out=x_grouped[:].rearrange("p (s f t) -> p s f t", s=S2, t=PACK),
-            in0=x_raw[:].rearrange("p t (f s) -> p s f t", s=S2),
-            scalar1=1.0,
-            scalar2=0.0,
-            op0=MULT,
-            op1=ADD,
+            in_=x_raw[:].rearrange("p t (f s) -> p s f t", s=S2),
         )
         x_words = keep.tile([P, S2 * F], U32, align_bytes=64)
         x_scales = keep.tile([P, S2 * F], U8, align_bytes=64)
+        nc.vector.quantize_mx(out=x_words[:].bitcast(E4M3X4), scales=x_scales[:], in_=x_grouped[:])
 
         def flip(chunk, first, count):
             bank = banks.tile([P, WINDOW], F32)
@@ -105,8 +98,6 @@ def tile_s2conv_pa_s_kernel(tc, x, psi, grad_out, out):
                         )
             g_words.append(words)
             g_scales.append(scales)
-            if gt == 0:
-                nc.vector.quantize_mx(out=x_words[:].bitcast(E4M3X4), scales=x_scales[:], in_=x_grouped[:])
 
         def multiply(acc, gt, s, first_c, start, stop):
             window = slice(first_c * P, first_c * P + WINDOW)

@@ -20,8 +20,6 @@ CHUNKS_PER_TILE = P // CHUNK_G
 G_TILES = G // P
 CHUNKS = G_TILES * CHUNKS_PER_TILE
 SCALAR_PAIRS = 3
-QUANT_CHUNKS = 2
-QUANT_G = QUANT_CHUNKS * CHUNK_G
 PSUM_BANKS = 8
 WINDOW = 4 * P
 
@@ -61,43 +59,41 @@ def tile_s2conv_pa_s_kernel(tc, x, psi, grad_out, out):
         x_scales = keep.tile([P, S2 * F], U8, align_bytes=64)
         nc.vector.quantize_mx(out=x_words[:].bitcast(E4M3X4), scales=x_scales[:], in_=x_grouped[:])
 
-        def flip(chunk, first, count):
-            bank = banks.tile([P, WINDOW], F32)
-            for j in range(count):
-                nc.tensor.transpose(bank[:, j * P : (j + 1) * P], chunk[:, first + j, :], ident[:])
-            return bank[:].bitcast(BF16)[:, : 2 * count * P].rearrange("p (w k e) -> p w e k", w=count, e=2)
-
+        g_grouped = []
         g_words = []
         g_scales = []
         for gt in range(G_TILES):
-            g_grouped = tiles.tile([P, C * P * PACK], BF16, align_bytes=64)
-            grouped_view = g_grouped[:].rearrange("p (w e g t) -> p w e g t", w=PAIRS, e=2, t=PACK)
-            words = tiles.tile([P, C * P], U32, align_bytes=64)
-            scales = tiles.tile([P, C * P], U8, align_bytes=64)
-            for i in range(CHUNKS_PER_TILE):
-                chunk = pair_cols[gt * CHUNKS_PER_TILE + i]
-                features = slice(i * CHUNK_G, (i + 1) * CHUNK_G)
-                for_scalar = flip(chunk, 0, SCALAR_PAIRS)
-                for_vector = flip(chunk, SCALAR_PAIRS, PAIRS - SCALAR_PAIRS)
-                nc.scalar.copy(
-                    out=grouped_view[:, :SCALAR_PAIRS, :, features, :].rearrange("p w e g t -> p w e (g t)"),
-                    in_=for_scalar,
-                )
-                nc.vector.tensor_copy(
-                    out=grouped_view[:, SCALAR_PAIRS:, :, features, :].rearrange("p w e g t -> p w e (g t)"),
-                    in_=for_vector,
-                )
-                if (i + 1) % QUANT_CHUNKS == 0:
-                    for c in range(C):
-                        first_col = c * P + (i + 1) * CHUNK_G - QUANT_G
-                        cols = slice(first_col, first_col + QUANT_G)
-                        nc.vector.quantize_mx(
-                            out=words[:, cols].bitcast(E5M2X4),
-                            scales=scales[:, cols],
-                            in_=g_grouped[:, first_col * PACK : (first_col + QUANT_G) * PACK],
-                        )
+            grouped = tiles.tile([P, C * P * PACK], BF16, align_bytes=64, tag="grouped")
+            words = tiles.tile([P, C * P], U32, align_bytes=64, tag="words")
+            scales = tiles.tile([P, C * P], U8, align_bytes=64, tag="scales")
+            g_grouped.append(grouped)
             g_words.append(words)
             g_scales.append(scales)
+
+        def flips(pool, tag, first_chunk, chunks, first_pair, pairs):
+            bank = pool.tile([P, WINDOW], F32, tag=tag)
+            for j in range(pairs):
+                for m in range(chunks):
+                    col = (j * chunks + m) * P
+                    nc.tensor.transpose(bank[:, col : col + P], pair_cols[first_chunk + m][:, first_pair + j, :], ident[:])
+            return bank[:].bitcast(BF16)[:, : 2 * pairs * chunks * P].rearrange("p (w k e) -> p w e k", w=pairs, e=2)
+
+        def regroup(copy, flipped, first_chunk, chunks, first_pair, pairs):
+            gt, i = divmod(first_chunk, CHUNKS_PER_TILE)
+            grouped_view = g_grouped[gt][:].rearrange("p (w e g t) -> p w e g t", w=PAIRS, e=2, t=PACK)
+            features = slice(i * CHUNK_G, (i + chunks) * CHUNK_G)
+            copy(
+                out=grouped_view[:, first_pair : first_pair + pairs, :, features, :].rearrange("p w e g t -> p w e (g t)"),
+                in_=flipped,
+            )
+
+        def quantise(gt, first_c, count):
+            cols = slice(first_c * P, (first_c + count) * P)
+            nc.vector.quantize_mx(
+                out=g_words[gt][:, cols].bitcast(E5M2X4),
+                scales=g_scales[gt][:, cols],
+                in_=g_grouped[gt][:, first_c * P * PACK : (first_c + count) * P * PACK],
+            )
 
         def multiply(acc, gt, s, first_c, start, stop):
             window = slice(first_c * P, first_c * P + WINDOW)
@@ -111,26 +107,68 @@ def tile_s2conv_pa_s_kernel(tc, x, psi, grad_out, out):
                 stop=stop,
             )
 
-        scaled_sums = []
-        for gt in range(G_TILES):
+        def chunk_flips(n):
+            return (
+                flips(banks, "bank", n, 1, 0, SCALAR_PAIRS),
+                flips(banks, "bank", n, 1, SCALAR_PAIRS, PAIRS - SCALAR_PAIRS),
+            )
+
+        def chunk_regroup(n, flipped):
+            regroup(nc.scalar.copy, flipped[0], n, 1, 0, SCALAR_PAIRS)
+            regroup(nc.vector.tensor_copy, flipped[1], n, 1, SCALAR_PAIRS, PAIRS - SCALAR_PAIRS)
+
+        for n in range(CHUNKS):
+            chunk_regroup(n, chunk_flips(n))
+            if n == 4:
+                quantise(0, 0, 8)
+            if n == 5:
+                quantise(0, 8, 2)
+        quantise(1, 0, 4)
+        quantise(1, 4, 4)
+        quantise(1, 8, 2)
+
+        def products(gt):
             acc0 = banks.tile([P, WINDOW], F32, tag="bank")
             multiply(acc0, gt, 0, 0, True, True)
             acc1 = banks.tile([P, WINDOW], F32, tag="bank")
             for u in range(3):
                 multiply(acc1, gt, 1 + u, 3 * u, u == 0, u == 2)
-            scaled = tiles.tile([P, S2 * P], F32)
-            nc.vector.tensor_scalar_mul(out=scaled[:, :P], in0=acc0[:, :P], scalar1=scale)
-            nc.scalar.mul(out=scaled[:, P:], in_=acc1[:, P:], mul=scale)
-            scaled_sums.append(scaled)
+            return (acc0, acc1)
 
-        for gt in range(G_TILES):
-            back = banks.tile([P, S2 * F], F32, tag="bank")
-            for s in range(S2):
-                nc.tensor.transpose(back[:, s * F : (s + 1) * F], scaled_sums[gt][:, s * P : (s + 1) * P], ident[:])
-            result = tiles.tile([P, F * S2], F32)
-            last_copy = nc.vector.tensor_copy if gt % 2 == 0 else nc.scalar.copy
-            last_copy(
-                out=result[:].rearrange("p (f s) -> p f s", s=S2),
-                in_=back[:].rearrange("p (s f) -> p f s", s=S2),
+        def flip_back(back, scaled, s):
+            nc.tensor.transpose(back[:, s * F : (s + 1) * F], scaled[:, s * P : (s + 1) * P], ident[:])
+
+        a_acc0, a_acc1 = products(0)
+        b_acc0, b_acc1 = products(1)
+
+        a_scaled = tiles.tile([P, S2 * P], F32, tag="scaled")
+        nc.scalar.mul(out=a_scaled[:, :P], in_=a_acc0[:, :P], mul=scale)
+        nc.scalar.mul(out=a_scaled[:, P:], in_=a_acc1[:, P:], mul=scale)
+        a_back = banks.tile([P, S2 * F], F32, tag="bank")
+        for s in range(S2):
+            flip_back(a_back, a_scaled, s)
+        a_result = tiles.tile([P, F * S2], F32, tag="result")
+        nc.scalar.copy(
+            out=a_result[:].rearrange("p (f s) -> p f s", s=S2),
+            in_=a_back[:].rearrange("p (s f) -> p f s", s=S2),
+        )
+        nc.sync.dma_start(out=out[0:P].rearrange("g f s -> g (f s)"), in_=a_result[:])
+
+        b_scaled = tiles.tile([P, S2 * P], F32, tag="scaled")
+        b_back = banks.tile([P, S2 * F], F32, tag="bank")
+        for s in range(S2):
+            acc = b_acc0 if s == 0 else b_acc1
+            nc.vector.tensor_scalar_mul(out=b_scaled[:, s * P : (s + 1) * P], in0=acc[:, s * P : (s + 1) * P], scalar1=scale)
+            flip_back(b_back, b_scaled, s)
+        b_result = tiles.tile([P, F * S2], F32, tag="result")
+        HALF_F = F // 2
+        for h in range(2):
+            features = slice(h * HALF_F, (h + 1) * HALF_F)
+            nc.vector.tensor_copy(
+                out=b_result[:].rearrange("p (f s) -> p f s", s=S2)[:, features, :],
+                in_=b_back[:].rearrange("p (s f) -> p f s", s=S2)[:, features, :],
             )
-            nc.sync.dma_start(out=out[gt * P : (gt + 1) * P].rearrange("g f s -> g (f s)"), in_=result[:])
+            nc.sync.dma_start(
+                out=out[P : 2 * P, features, :].rearrange("g f s -> g (f s)"),
+                in_=b_result[:, h * HALF_F * S2 : (h + 1) * HALF_F * S2],
+            )

@@ -117,29 +117,41 @@ def tile_s2conv_pa_s_kernel(tc, x, psi, grad_out, out):
             regroup(nc.scalar.copy, flipped[0], n, 1, 0, SCALAR_PAIRS)
             regroup(nc.vector.tensor_copy, flipped[1], n, 1, SCALAR_PAIRS, PAIRS - SCALAR_PAIRS)
 
-        for n in range(CHUNKS):
+        idle_bank = banks.tile([P, P], F32, tag="bank")
+        for i in range(3):
+            nc.tensor.matmul(idle_bank[:], lhsT=ident[:], rhs=ident[:], start=True, stop=True)
+        for n in range(CHUNKS - 2):
             chunk_regroup(n, chunk_flips(n))
             if n == 4:
                 quantise(0, 0, 8)
             if n == 5:
                 quantise(0, 8, 2)
+        LAST = CHUNKS - 2
+        pairs_01 = flips(banks, "bank", LAST, 2, 0, 2)
+        pair_4 = flips(banks, "bank", LAST, 2, 4, 1)
+        pair_3 = flips(banks, "bank", LAST, 2, 3, 1)
+        pair_2 = flips(banks, "bank", LAST, 2, 2, 1)
+        regroup(nc.scalar.copy, pairs_01, LAST, 2, 0, 2)
+        regroup(nc.vector.tensor_copy, pair_4, LAST, 2, 4, 1)
+        regroup(nc.scalar.copy, pair_3, LAST, 2, 3, 1)
+        regroup(nc.scalar.copy, pair_2, LAST, 2, 2, 1)
         quantise(1, 0, 4)
-        quantise(1, 4, 4)
-        quantise(1, 8, 2)
+        quantise(1, 6, 4)
+        quantise(1, 4, 2)
 
-        def products(gt):
+        def products(gt, order):
             acc0 = banks.tile([P, WINDOW], F32, tag="bank")
             multiply(acc0, gt, 0, 0, True, True)
             acc1 = banks.tile([P, WINDOW], F32, tag="bank")
-            for u in range(3):
-                multiply(acc1, gt, 1 + u, 3 * u, u == 0, u == 2)
+            for u in order:
+                multiply(acc1, gt, 1 + u, 3 * u, u == order[0], u == order[2])
             return (acc0, acc1)
 
         def flip_back(back, scaled, s):
             nc.tensor.transpose(back[:, s * F : (s + 1) * F], scaled[:, s * P : (s + 1) * P], ident[:])
 
-        a_acc0, a_acc1 = products(0)
-        b_acc0, b_acc1 = products(1)
+        a_acc0, a_acc1 = products(0, (0, 1, 2))
+        b_acc0, b_acc1 = products(1, (0, 2, 1))
 
         a_scaled = tiles.tile([P, S2 * P], F32, tag="scaled")
         nc.scalar.mul(out=a_scaled[:, :P], in_=a_acc0[:, :P], mul=scale)

@@ -121,16 +121,32 @@ def tile_s2conv_pa_s_kernel(tc, x, psi, grad_out, out):
         for i in range(3):
             nc.tensor.matmul(idle_bank[:], lhsT=ident[:], rhs=ident[:], start=True, stop=True)
         for n in range(CHUNKS - 2):
-            chunk_regroup(n, chunk_flips(n))
+            if n == 1:
+                two_pairs = flips(banks, "bank", n, 1, 0, 2)
+                three_pairs = flips(banks, "bank", n, 1, 2, 3)
+                regroup(nc.scalar.copy, two_pairs, n, 1, 0, 2)
+                regroup(nc.vector.tensor_copy, three_pairs, n, 1, 2, 3)
+            else:
+                chunk_regroup(n, chunk_flips(n))
             if n == 4:
                 quantise(0, 0, 8)
             if n == 5:
                 quantise(0, 8, 2)
         LAST = CHUNKS - 2
-        pairs_01 = flips(banks, "bank", LAST, 2, 0, 2)
-        pair_4 = flips(banks, "bank", LAST, 2, 4, 1)
-        pair_3 = flips(banks, "bank", LAST, 2, 3, 1)
-        pair_2 = flips(banks, "bank", LAST, 2, 2, 1)
+        jobs = ((0, 2), (4, 1), (3, 1), (2, 1))
+        job_banks = []
+        for job in jobs:
+            bank = banks.tile([P, WINDOW], F32, tag="bank")
+            job_banks.append(bank)
+        for m in range(2):
+            for (first_pair, pairs), bank in zip(jobs, job_banks):
+                for j in range(pairs):
+                    col = (j * 2 + m) * P
+                    nc.tensor.transpose(bank[:, col : col + P], pair_cols[LAST + m][:, first_pair + j, :], ident[:])
+        pairs_01, pair_4, pair_3, pair_2 = [
+            bank[:].bitcast(BF16)[:, : 4 * pairs * P].rearrange("p (w k e) -> p w e k", w=pairs, e=2)
+            for (first_pair, pairs), bank in zip(jobs, job_banks)
+        ]
         regroup(nc.scalar.copy, pairs_01, LAST, 2, 0, 2)
         regroup(nc.vector.tensor_copy, pair_4, LAST, 2, 4, 1)
         regroup(nc.scalar.copy, pair_3, LAST, 2, 3, 1)

import math
from contextlib import ExitStack

import concourse.mybir as mybir
from concourse.masks import make_identity

F32 = mybir.dt.float32
BF16 = mybir.dt.bfloat16
U32 = mybir.dt.uint32
U8 = mybir.dt.uint8
E4M3X4 = mybir.dt.float8_e4m3fn_x4
E5M2X4 = mybir.dt.float8_e5m2_x4

P = 128
PACK = 4
B, F, G, S2, C = 512, 128, 256, 4, 10
PAIRS = C // 2
CHUNK_G = P // PACK
CHUNKS_PER_TILE = P // CHUNK_G
G_TILES = G // P
CHUNKS = G_TILES * CHUNKS_PER_TILE
SCALAR_PAIRS = 3
PSUM_BANKS = 8
WINDOW = 4 * P

FLOPS = 2 * B * F * G * C
BYTES = 2 * B * F * S2 + 2 * G * B * C + 4 * G * F * S2


def tile_s2conv_pa_s_kernel(tc, x, psi, grad_out, out):
    nc = tc.nc
    scale = 1.0 / math.sqrt(F)

    with ExitStack() as ctx:
        keep = ctx.enter_context(tc.tile_pool(name="keep", bufs=1))
        loads = ctx.enter_context(tc.tile_pool(name="loads", bufs=CHUNKS))
        tiles = ctx.enter_context(tc.tile_pool(name="tiles", bufs=G_TILES))
        banks = ctx.enter_context(tc.psum_pool(name="banks", bufs=PSUM_BANKS))
        ctx.enter_context(tc.manual_schedule())

        ident = keep.tile([P, P], F32)
        make_identity(nc, ident[:])

        chunk_rows = grad_out.rearrange("(n g) (t b) c -> n (g t) (b c)", g=CHUNK_G, t=PACK)
        x_raw = keep.tile([P, PACK, F * S2], BF16)
        nc.sync.dma_start(out=x_raw[:], in_=x.rearrange("(t p) f s -> p t (f s)", p=P))
        pair_cols = []
        for n in range(CHUNKS):
            raw = loads.tile([P, P * C], BF16)
            nc.sync.dma_start(out=raw[:], in_=chunk_rows[n])
            pair_cols.append(raw[:].bitcast(F32).rearrange("q (b w) -> q w b", w=PAIRS))

        x_grouped = keep.tile([P, S2 * F * PACK], BF16, align_bytes=64)
        nc.vector.tensor_copy(
            out=x_grouped[:].rearrange("p (s f t) -> p s f t", s=S2, t=PACK),
            in_=x_raw[:].rearrange("p t (f s) -> p s f t", s=S2),
        )
        x_words = keep.tile([P, S2 * F], U32, align_bytes=64)
        x_scales = keep.tile([P, S2 * F], U8, align_bytes=64)
        nc.vector.quantize_mx(out=x_words[:].bitcast(E4M3X4), scales=x_scales[:], in_=x_grouped[:])

        g_grouped = []
        g_words = []
        g_scales = []
        for gt in range(G_TILES):
            grouped = tiles.tile([P, C * P * PACK], BF16, align_bytes=64, tag="grouped")
            words = tiles.tile([P, C * P], U32, align_bytes=64, tag="words")
            scales = tiles.tile([P, C * P], U8, align_bytes=64, tag="scales")
            g_grouped.append(grouped)
            g_words.append(words)
            g_scales.append(scales)

        def flips(pool, tag, first_chunk, chunks, first_pair, pairs):
            bank = pool.tile([P, WINDOW], F32, tag=tag)
            for j in range(pairs):
                for m in range(chunks):
                    col = (j * chunks + m) * P
                    nc.tensor.transpose(bank[:, col : col + P], pair_cols[first_chunk + m][:, first_pair + j, :], ident[:])
            return bank[:].bitcast(BF16)[:, : 2 * pairs * chunks * P].rearrange("p (w k e) -> p w e k", w=pairs, e=2)

        def regroup(copy, flipped, first_chunk, chunks, first_pair, pairs):
            gt, i = divmod(first_chunk, CHUNKS_PER_TILE)
            grouped_view = g_grouped[gt][:].rearrange("p (w e g t) -> p w e g t", w=PAIRS, e=2, t=PACK)
            features = slice(i * CHUNK_G, (i + chunks) * CHUNK_G)
            copy(
                out=grouped_view[:, first_pair : first_pair + pairs, :, features, :].rearrange("p w e g t -> p w e (g t)"),
                in_=flipped,
            )

        def quantise(gt, first_c, count):
            cols = slice(first_c * P, (first_c + count) * P)
            nc.vector.quantize_mx(
                out=g_words[gt][:, cols].bitcast(E5M2X4),
                scales=g_scales[gt][:, cols],
                in_=g_grouped[gt][:, first_c * P * PACK : (first_c + count) * P * PACK],
            )

        def multiply(acc, gt, s, first_c, start, stop):
            window = slice(first_c * P, first_c * P + WINDOW)
            nc.tensor.matmul_mx(
                out=acc[:],
                lhsT=x_words[:, s * F : (s + 1) * F].bitcast(E4M3X4),
                lhsT_scale=x_scales[:, s * F : (s + 1) * F],
                rhs=g_words[gt][:, window].bitcast(E5M2X4),
                rhs_scale=g_scales[gt][:, window],
                start=start,
                stop=stop,
            )

        def chunk_flips(n):
            return (
                flips(banks, "bank", n, 1, 0, SCALAR_PAIRS),
                flips(banks, "bank", n, 1, SCALAR_PAIRS, PAIRS - SCALAR_PAIRS),
            )

        def chunk_regroup(n, flipped):
            regroup(nc.scalar.copy, flipped[0], n, 1, 0, SCALAR_PAIRS)
            regroup(nc.vector.tensor_copy, flipped[1], n, 1, SCALAR_PAIRS, PAIRS - SCALAR_PAIRS)

        idle_bank = banks.tile([P, P], F32, tag="bank")
        for i in range(3):
            nc.tensor.matmul(idle_bank[:], lhsT=ident[:], rhs=ident[:], start=True, stop=True)
        for n in range(CHUNKS - 2):
            if n == 1:
                two_pairs = flips(banks, "bank", n, 1, 0, 2)
                three_pairs = flips(banks, "bank", n, 1, 2, 3)
                regroup(nc.scalar.copy, two_pairs, n, 1, 0, 2)
                regroup(nc.vector.tensor_copy, three_pairs, n, 1, 2, 3)
            else:
                chunk_regroup(n, chunk_flips(n))
            if n == 4:
                quantise(0, 0, 8)
            if n == 5:
                quantise(0, 8, 2)
        LAST = CHUNKS - 2
        jobs = ((0, 2), (4, 1), (3, 1), (2, 1))
        job_banks = []
        for job in jobs:
            bank = banks.tile([P, WINDOW], F32, tag="bank")
            job_banks.append(bank)
        for m in range(2):
            for (first_pair, pairs), bank in zip(jobs, job_banks):
                for j in range(pairs):
                    col = (j * 2 + m) * P
                    nc.tensor.transpose(bank[:, col : col + P], pair_cols[LAST + m][:, first_pair + j, :], ident[:])
        pairs_01, pair_4, pair_3, pair_2 = [
            bank[:].bitcast(BF16)[:, : 4 * pairs * P].rearrange("p (w k e) -> p w e k", w=pairs, e=2)
            for (first_pair, pairs), bank in zip(jobs, job_banks)
        ]
        regroup(nc.scalar.copy, pairs_01, LAST, 2, 0, 2)
        regroup(nc.vector.tensor_copy, pair_4, LAST, 2, 4, 1)
        regroup(nc.scalar.copy, pair_3, LAST, 2, 3, 1)
        regroup(nc.scalar.copy, pair_2, LAST, 2, 2, 1)
        quantise(1, 0, 4)
        quantise(1, 6, 4)
        quantise(1, 4, 2)

        def products(gt, order):
            acc0 = banks.tile([P, WINDOW], F32, tag="bank")
            multiply(acc0, gt, 0, 0, True, True)
            acc1 = banks.tile([P, WINDOW], F32, tag="bank")
            for u in order:
                multiply(acc1, gt, 1 + u, 3 * u, u == order[0], u == order[2])
            return (acc0, acc1)

        def flip_back(back, scaled, s):
            nc.tensor.transpose(back[:, s * F : (s + 1) * F], scaled[:, s * P : (s + 1) * P], ident[:])

        a_acc0, a_acc1 = products(0, (0, 1, 2))
        b_acc0, b_acc1 = products(1, (0, 2, 1))

        a_scaled = tiles.tile([P, S2 * P], F32, tag="scaled")
        nc.scalar.mul(out=a_scaled[:, :P], in_=a_acc0[:, :P], mul=scale)
        nc.scalar.mul(out=a_scaled[:, P:], in_=a_acc1[:, P:], mul=scale)
        a_back = banks.tile([P, S2 * F], F32, tag="bank")
        for s in range(S2):
            flip_back(a_back, a_scaled, s)
        a_result = tiles.tile([P, F * S2], F32, tag="result")
        nc.scalar.copy(
            out=a_result[:].rearrange("p (f s) -> p f s", s=S2),
            in_=a_back[:].rearrange("p (s f) -> p f s", s=S2),
        )
        nc.sync.dma_start(out=out[0:P].rearrange("g f s -> g (f s)"), in_=a_result[:])

        b_scaled = tiles.tile([P, S2 * P], F32, tag="scaled")
        b_back = banks.tile([P, S2 * F], F32, tag="bank")
        for s in range(S2):
            acc = b_acc0 if s == 0 else b_acc1
            nc.vector.tensor_scalar_mul(out=b_scaled[:, s * P : (s + 1) * P], in0=acc[:, s * P : (s + 1) * P], scalar1=scale)
            flip_back(b_back, b_scaled, s)
        b_result = tiles.tile([P, F * S2], F32, tag="result")
        HALF_F = F // 2
        for h in range(2):
            features = slice(h * HALF_F, (h + 1) * HALF_F)
            nc.vector.tensor_copy(
                out=b_result[:].rearrange("p (f s) -> p f s", s=S2)[:, features, :],
                in_=b_back[:].rearrange("p (s f) -> p f s", s=S2)[:, features, :],
            )
            nc.sync.dma_start(
                out=out[P : 2 * P, features, :].rearrange("g f s -> g (f s)"),
                in_=b_result[:, h * HALF_F * S2 : (h + 1) * HALF_F * S2],
            )
